import numpy as np
import ml_dtypes


def mxq(x, axis, fmt="e4m3"):
    dtype, down = {"e4m3": (ml_dtypes.float8_e4m3fn, 7), "e5m2": (ml_dtypes.float8_e5m2, 14)}[fmt]
    v = np.moveaxis(np.asarray(x, np.float32).astype(ml_dtypes.bfloat16).astype(np.float64), axis, -1)
    blocks = v.reshape(v.shape[:-1] + (-1, 32))
    amax = np.abs(blocks).max(-1, keepdims=True)
    byte = np.maximum(np.where(amax > 0, np.frexp(amax)[1] - 1 + 127, 0) - down, 1)
    scale = np.exp2(byte - 127.0)
    codes = (blocks / scale).astype(np.float32).astype(dtype).astype(np.float64)
    return np.moveaxis((codes * scale).reshape(v.shape), -1, axis)


WIDE = False


def mx_kscale(k):
    if not WIDE:
        return np.ones(k)
    levels = np.array([10, -10, 5, -5, 0])
    a = np.random.permutation(np.resize(levels, k // 512 * 4)).reshape(k // 512, 4)
    idx = np.arange(k)
    return np.exp2(a[idx // 512, idx % 128 // 32])


BF16 = ml_dtypes.bfloat16


def bf(x):
    return np.asarray(x, np.float32).astype(BF16)


def f64(x):
    return np.asarray(x).astype(np.float64)


E2M1 = np.array([0.0, 0.5, 1.0, 1.5, 2.0, 3.0, 4.0, 6.0, -0.0, -0.5, -1.0, -1.5, -2.0, -3.0, -4.0, -6.0])


def pack_weight(w, fmt):
    k, n = w.shape
    w = f64(bf(w)).reshape(k // 32, 32, n)
    amax = np.abs(w).max(1)
    if fmt == "e4m3":
        byte = np.frexp(amax)[1] - 1 + 127 - 7
    else:
        mant, ex = np.frexp(amax / 6.0)
        byte = np.where(mant > 0.5, ex, ex - 1) + 127
    byte = np.clip(np.where(amax > 0, byte, 1), 1, 254)
    scaled = (w * np.exp2(127.0 - byte)[:, None, :]).reshape(k, n).astype(np.float32)
    by_word = np.ascontiguousarray(scaled.reshape(k // 512, 128, 4, n).transpose(0, 1, 3, 2))
    if fmt == "e4m3":
        words = by_word.astype(ml_dtypes.float8_e4m3fn).view(np.uint8)
    else:
        c = by_word.astype(ml_dtypes.float4_e2m1fn).view(np.uint8) & 0xF
        words = c[..., 0::2] | (c[..., 1::2] << 4)
    return np.ascontiguousarray(words), np.ascontiguousarray(byte.astype(np.uint8).reshape(k // 512, 16, n))


def unpack_weight(words, scales, fmt):
    g, p, n, _ = words.shape
    if fmt == "e4m3":
        vals = np.ascontiguousarray(words).view(ml_dtypes.float8_e4m3fn).astype(np.float64)
    else:
        nib = np.empty((g, p, n, 4), np.uint8)
        nib[..., 0::2] = words & 0xF
        nib[..., 1::2] = words >> 4
        vals = E2M1[nib]
    vals = vals * np.repeat(np.exp2(scales.astype(np.float64) - 127.0), 8, axis=1)[..., None]
    return vals.transpose(0, 1, 3, 2).reshape(g * 512, n)


N, C, F, G = 128, 3, 512, 16384
F2 = F + F
F3 = F2 + F
FMT = "e4m3"


def silu(v):
    return v / (1.0 + np.exp(-v))


def setup_inputs():
    s = mx_kscale(G)
    h = bf(silu(1.4 * np.random.standard_normal((N, 1, G))) * s)
    mu_W = bf(np.random.standard_normal((N, C, F)))
    mu_VW = bf(np.sqrt(C) * np.random.standard_normal((N, 1, F)))
    q = bf(np.random.standard_normal((N, 1, F)))
    mu = bf(np.random.standard_normal((N, C, F)))
    W2 = np.random.standard_normal((F3, G)) / np.sqrt(G) / s
    words, scales = pack_weight(np.ascontiguousarray(W2.T), FMT)
    b2 = bf(0.2 * np.random.standard_normal(F3))
    return {"h": h,
            "mu_W": mu_W,
            "mu_VW": mu_VW,
            "q": q,
            "mu": mu,
            "W2_words": words,
            "W2_scales": scales,
            "b2": b2}


def reference(h, mu_W, mu_VW, q, mu, W2_words, W2_scales, b2):
    x = (mxq(f64(h), 2, "e4m3") @ unpack_weight(W2_words, W2_scales, FMT)) + f64(b2)
    dq_intra = x[..., :F]
    dmu_intra = x[..., F:F2] * f64(mu_W)
    dqmu_intra = x[..., F2:] * f64(mu_VW)
    q_out = f64(q) + dq_intra + dqmu_intra
    mu_out = f64(mu) + dmu_intra
    return q_out, mu_out

@@ -1,0 +1,202 @@
+from contextlib import ExitStack
+
+import concourse.mybir as mybir
+from concourse.masks import make_identity
+
+F32 = mybir.dt.float32
+BF16 = mybir.dt.bfloat16
+I32 = mybir.dt.int32
+U32 = mybir.dt.uint32
+U8 = mybir.dt.uint8
+FP8X4 = mybir.dt.float8_e4m3fn_x4
+MULT = mybir.AluOpType.mult
+ADD = mybir.AluOpType.add
+
+P = 128
+K = 16384
+K_PASS = 512
+GROUPS = K // K_PASS
+F = 512
+BLOCKS = 3
+COMPONENTS = 3
+
+CHUNK_GROUPS = 8
+CHUNKS = GROUPS // CHUNK_GROUPS
+WORDS_PER_GROUP = K_PASS // 2
+PLANES_PER_TILE = 4
+SETS = GROUPS // PLANES_PER_TILE
+QUADRANTS = 4
+
+TAIL_GROUPS = 4
+TAIL_BLOCK_ORDER = (1, 2, 0)
+W_RING = 12
+
+FLOPS = 2 * P * K * BLOCKS * F
+
+
+def tile_painnmixing_pb_k_kernel(
+    tc, h, mu_W, mu_VW, q, mu, W2_words, W2_scales, b2, out_0, out_1
+):
+    nc = tc.nc
+    h_flat = h.rearrange("n o k -> n (o k)")
+    with ExitStack() as ctx:
+        ctx.enter_context(tc.manual_schedule())
+        keep = ctx.enter_context(tc.tile_pool(name="keep", bufs=1))
+        h_pool = ctx.enter_context(tc.tile_pool(name="h_pool", bufs=CHUNKS))
+        grouped_pool = ctx.enter_context(tc.tile_pool(name="grouped_pool", bufs=2))
+        w_pool = ctx.enter_context(tc.tile_pool(name="w_pool", bufs=W_RING))
+        tail_pool = ctx.enter_context(
+            tc.tile_pool(name="tail_pool", bufs=TAIL_GROUPS * BLOCKS)
+        )
+        work_psum = ctx.enter_context(tc.psum_pool(name="work_psum", bufs=4))
+        acc_psum = ctx.enter_context(tc.psum_pool(name="acc_psum", bufs=1))
+
+        w_planes = keep.tile([P, SETS, BLOCKS * F], U8, align_bytes=64)
+        nc.vector.memset(w_planes[:].bitcast(I32), 0)
+        bias_rows = keep.tile([P, BLOCKS * F], BF16)
+        nc.vector.memset(bias_rows[:], 0.0)
+        ones = keep.tile([P, P], BF16)
+        nc.vector.memset(ones[:], 1.0)
+        identity = keep.tile([P, P], F32)
+        make_identity(nc, identity[:])
+
+        h_chunks = []
+        for c in range(CHUNKS):
+            h_raw = h_pool.tile([P, CHUNK_GROUPS * K_PASS], BF16)
+            cols = slice(c * CHUNK_GROUPS * K_PASS, (c + 1) * CHUNK_GROUPS * K_PASS)
+            nc.sync.dma_start(out=h_raw[:], in_=h_flat[:, cols])
+            h_chunks.append(h_raw)
+
+        for s in range(SETS):
+            for quad in range(QUADRANTS):
+                nc.sync.dma_start(
+                    out=w_planes[32 * quad : 32 * quad + 16, s, :].bitcast(I32),
+                    in_=W2_scales[
+                        PLANES_PER_TILE * s : PLANES_PER_TILE * (s + 1),
+                        4 * quad : 4 * quad + 4,
+                        :,
+                    ].bitcast(I32),
+                )
+
+        nc.sync.dma_start(out=bias_rows[0:1, :], in_=b2.unsqueeze(0))
+        q_in = keep.tile([P, F], BF16)
+        nc.sync.dma_start(out=q_in[:], in_=q.rearrange("n o f -> n (o f)"))
+        mu_vw_in = keep.tile([P, F], BF16)
+        nc.sync.dma_start(out=mu_vw_in[:], in_=mu_VW.rearrange("n o f -> n (o f)"))
+        mu_w_in = keep.tile([P, COMPONENTS, F], BF16)
+        nc.sync.dma_start(out=mu_w_in[:], in_=mu_W)
+        mu_in = keep.tile([P, COMPONENTS, F], BF16)
+        nc.sync.dma_start(out=mu_in[:], in_=mu)
+
+        h_codes = keep.tile([P, GROUPS * P], U32, align_bytes=64)
+        h_planes = keep.tile([P, GROUPS * P], U8, align_bytes=64)
+        for c in range(CHUNKS):
+            h_words = h_chunks[c][:].bitcast(F32)
+            grouped = grouped_pool.tile([P, CHUNK_GROUPS * K_PASS], BF16, align_bytes=64)
+            grouped_words = grouped[:].bitcast(F32)
+            for pair in range(CHUNK_GROUPS // 2):
+                flipped = work_psum.tile([P, 2, 2, P], F32, tag="work")
+                for i in range(2):
+                    first = (2 * pair + i) * WORDS_PER_GROUP
+                    for u in range(2):
+                        nc.tensor.transpose(
+                            flipped[:, i, u, :],
+                            h_words[:, first + u : first + WORDS_PER_GROUP : 2],
+                            identity[:],
+                        )
+                target = grouped_words[
+                    :, 2 * pair * WORDS_PER_GROUP : 2 * (pair + 1) * WORDS_PER_GROUP
+                ].rearrange("p (i n u) -> p i n u", i=2, u=2)
+                source = flipped[:].rearrange("p i u n -> p i n u")
+                if pair % 2 == 0:
+                    nc.vector.tensor_copy(out=target, in_=source)
+                else:
+                    nc.scalar.copy(out=target, in_=source)
+            chunk_cols = slice(c * CHUNK_GROUPS * P, (c + 1) * CHUNK_GROUPS * P)
+            nc.vector.quantize_mx(
+                out=h_codes[:, chunk_cols].bitcast(FP8X4),
+                scales=h_planes[:, chunk_cols],
+                in_=grouped[:],
+            )
+
+        bias = []
+        for b in range(BLOCKS):
+            bias_b = work_psum.tile([P, F], F32, tag="work")
+            nc.tensor.matmul(
+                bias_b[:], lhsT=ones[:], rhs=bias_rows[:, b * F : (b + 1) * F],
+                start=True, stop=True,
+            )
+            bias.append(bias_b)
+        base_q = keep.tile([P, F], F32)
+        gated = keep.tile([P, F], F32)
+        nc.vector.tensor_tensor(out=base_q[:], in0=bias[0][:], in1=q_in[:], op=ADD)
+        nc.vector.tensor_tensor(out=gated[:], in0=bias[2][:], in1=mu_vw_in[:], op=MULT)
+        nc.vector.tensor_tensor(out=base_q[:], in0=base_q[:], in1=gated[:], op=ADD)
+        base_mu = keep.tile([P, COMPONENTS, F], F32)
+        for x in range(COMPONENTS):
+            nc.vector.tensor_tensor(
+                out=base_mu[:, x, :], in0=bias[1][:], in1=mu_w_in[:, x, :], op=MULT
+            )
+            nc.vector.tensor_tensor(
+                out=base_mu[:, x, :], in0=base_mu[:, x, :], in1=mu_in[:, x, :], op=ADD
+            )
+
+        acc = [acc_psum.tile([P, F], F32, name="acc%d" % b) for b in range(BLOCKS)]
+
+        def mx_pass(g, b, w_words):
+            first_row = 4 * (g % PLANES_PER_TILE)
+            nc.tensor.matmul_mx(
+                out=acc[b][:],
+                lhsT=h_codes[:, g * P : (g + 1) * P].bitcast(FP8X4),
+                lhsT_scale=h_planes[:, g * P : (g + 1) * P],
+                rhs=w_words.bitcast(FP8X4),
+                rhs_scale=w_planes[first_row:P, g // PLANES_PER_TILE, b * F : (b + 1) * F],
+                start=(g == 0),
+                stop=(g == GROUPS - 1),
+            )
+
+        for g in range(GROUPS - TAIL_GROUPS):
+            w_group = w_pool.tile([P, BLOCKS * F], U32, align_bytes=64)
+            nc.sync.dma_start(
+                out=w_group[:].bitcast(I32),
+                in_=W2_words[g].rearrange("p n t -> p (n t)").bitcast(I32),
+            )
+            for b in range(BLOCKS):
+                mx_pass(g, b, w_group[:, b * F : (b + 1) * F])
+
+        tail_groups = range(GROUPS - TAIL_GROUPS, GROUPS)
+        tail_words = {}
+        for b in TAIL_BLOCK_ORDER:
+            for g in tail_groups:
+                w_part = tail_pool.tile([P, F], U32, align_bytes=64)
+                nc.sync.dma_start(
+                    out=w_part[:].bitcast(I32),
+                    in_=W2_words[g][:, b * F : (b + 1) * F, :]
+                    .rearrange("p n t -> p (n t)")
+                    .bitcast(I32),
+                )
+                tail_words[(b, g)] = w_part
+
+        for g in tail_groups:
+            mx_pass(g, 1, tail_words[(1, g)][:])
+        mu_prod = keep.tile([P, COMPONENTS, F], F32)
+        mu_res = keep.tile([P, COMPONENTS, F], F32)
+        for x in range(COMPONENTS):
+            nc.vector.tensor_tensor(
+                out=mu_prod[:, x, :], in0=acc[1][:], in1=mu_w_in[:, x, :], op=MULT
+            )
+            nc.gpsimd.tensor_tensor(
+                out=mu_res[:, x, :], in0=mu_prod[:, x, :], in1=base_mu[:, x, :], op=ADD
+            )
+            nc.sync.dma_start(out=out_1[:, x, :], in_=mu_res[:, x, :])
+
+        for g in tail_groups:
+            mx_pass(g, 2, tail_words[(2, g)][:])
+        nc.vector.tensor_tensor(out=gated[:], in0=acc[2][:], in1=mu_vw_in[:], op=MULT)
+        nc.vector.tensor_tensor(out=base_q[:], in0=base_q[:], in1=gated[:], op=ADD)
+
+        for g in tail_groups:
+            mx_pass(g, 0, tail_words[(0, g)][:])
+        q_res = keep.tile([P, F], F32)
+        nc.vector.tensor_tensor(out=q_res[:], in0=acc[0][:], in1=base_q[:], op=ADD)
+        nc.sync.dma_start(out=out_0.rearrange("n o f -> n (o f)"), in_=q_res[:])

@@ -157,10 +157,16 @@ def tile_painnmixing_pb_k_kernel(
 
         for g in range(GROUPS - TAIL_GROUPS):
             w_group = w_pool.tile([P, BLOCKS * F], U32, align_bytes=64)
-            nc.sync.dma_start(
-                out=w_group[:].bitcast(I32),
-                in_=W2_words[g].rearrange("p n t -> p (n t)").bitcast(I32),
-            )
+            if g % 2 == 0:
+                nc.sync.dma_start(
+                    out=w_group[:].bitcast(I32),
+                    in_=W2_words[g].rearrange("p n t -> p (n t)").bitcast(I32),
+                )
+            else:
+                nc.scalar.dma_start(
+                    out=w_group[:].bitcast(F32),
+                    in_=W2_words[g].rearrange("p n t -> p (n t)").bitcast(F32),
+                )
             for b in range(BLOCKS):
                 mx_pass(g, b, w_group[:, b * F : (b + 1) * F])
 

@@ -26,6 +26,7 @@ WORDS_PER_GROUP = K_PASS // 2
 PLANES_PER_TILE = 4
 SETS = GROUPS // PLANES_PER_TILE
 QUADRANTS = 4
+QUADRANT_ORDER = (0, 2, 1, 3)
 
 TAIL_GROUPS = 4
 TAIL_BLOCK_ORDER = (1, 2, 0)
@@ -68,7 +69,7 @@ def tile_painnmixing_pb_k_kernel(
             h_chunks.append(h_raw)
 
         for s in range(SETS):
-            for quad in range(QUADRANTS):
+            for quad in QUADRANT_ORDER:
                 nc.sync.dma_start(
                     out=w_planes[32 * quad : 32 * quad + 16, s, :].bitcast(I32),
                     in_=W2_scales[

from contextlib import ExitStack

import concourse.mybir as mybir
from concourse.masks import make_identity

F32 = mybir.dt.float32
BF16 = mybir.dt.bfloat16
I32 = mybir.dt.int32
U32 = mybir.dt.uint32
U8 = mybir.dt.uint8
FP8X4 = mybir.dt.float8_e4m3fn_x4
MULT = mybir.AluOpType.mult
ADD = mybir.AluOpType.add

P = 128
K = 16384
K_PASS = 512
GROUPS = K // K_PASS
F = 512
BLOCKS = 3
COMPONENTS = 3

CHUNK_GROUPS = 8
CHUNKS = GROUPS // CHUNK_GROUPS
WORDS_PER_GROUP = K_PASS // 2
PLANES_PER_TILE = 4
SETS = GROUPS // PLANES_PER_TILE
QUADRANTS = 4
QUADRANT_ORDER = (0, 2, 1, 3)

TAIL_GROUPS = 4
TAIL_BLOCK_ORDER = (1, 2, 0)
W_RING = 12

FLOPS = 2 * P * K * BLOCKS * F


def tile_painnmixing_pb_k_kernel(
    tc, h, mu_W, mu_VW, q, mu, W2_words, W2_scales, b2, out_0, out_1
):
    nc = tc.nc
    h_flat = h.rearrange("n o k -> n (o k)")
    with ExitStack() as ctx:
        ctx.enter_context(tc.manual_schedule())
        keep = ctx.enter_context(tc.tile_pool(name="keep", bufs=1))
        h_pool = ctx.enter_context(tc.tile_pool(name="h_pool", bufs=CHUNKS))
        grouped_pool = ctx.enter_context(tc.tile_pool(name="grouped_pool", bufs=2))
        w_pool = ctx.enter_context(tc.tile_pool(name="w_pool", bufs=W_RING))
        tail_pool = ctx.enter_context(
            tc.tile_pool(name="tail_pool", bufs=TAIL_GROUPS * BLOCKS)
        )
        work_psum = ctx.enter_context(tc.psum_pool(name="work_psum", bufs=4))
        acc_psum = ctx.enter_context(tc.psum_pool(name="acc_psum", bufs=1))

        w_planes = keep.tile([P, SETS, BLOCKS * F], U8, align_bytes=64)
        nc.vector.memset(w_planes[:].bitcast(I32), 0)
        bias_rows = keep.tile([P, BLOCKS * F], BF16)
        nc.vector.memset(bias_rows[:], 0.0)
        ones = keep.tile([P, P], BF16)
        nc.vector.memset(ones[:], 1.0)
        identity = keep.tile([P, P], F32)
        make_identity(nc, identity[:])

        h_chunks = []
        for c in range(CHUNKS):
            h_raw = h_pool.tile([P, CHUNK_GROUPS * K_PASS], BF16)
            cols = slice(c * CHUNK_GROUPS * K_PASS, (c + 1) * CHUNK_GROUPS * K_PASS)
            nc.sync.dma_start(out=h_raw[:], in_=h_flat[:, cols])
            h_chunks.append(h_raw)

        for s in range(SETS):
            for quad in QUADRANT_ORDER:
                nc.sync.dma_start(
                    out=w_planes[32 * quad : 32 * quad + 16, s, :].bitcast(I32),
                    in_=W2_scales[
                        PLANES_PER_TILE * s : PLANES_PER_TILE * (s + 1),
                        4 * quad : 4 * quad + 4,
                        :,
                    ].bitcast(I32),
                )

        nc.sync.dma_start(out=bias_rows[0:1, :], in_=b2.unsqueeze(0))
        q_in = keep.tile([P, F], BF16)
        nc.sync.dma_start(out=q_in[:], in_=q.rearrange("n o f -> n (o f)"))
        mu_vw_in = keep.tile([P, F], BF16)
        nc.sync.dma_start(out=mu_vw_in[:], in_=mu_VW.rearrange("n o f -> n (o f)"))
        mu_w_in = keep.tile([P, COMPONENTS, F], BF16)
        nc.sync.dma_start(out=mu_w_in[:], in_=mu_W)
        mu_in = keep.tile([P, COMPONENTS, F], BF16)
        nc.sync.dma_start(out=mu_in[:], in_=mu)

        h_codes = keep.tile([P, GROUPS * P], U32, align_bytes=64)
        h_planes = keep.tile([P, GROUPS * P], U8, align_bytes=64)
        for c in range(CHUNKS):
            h_words = h_chunks[c][:].bitcast(F32)
            grouped = grouped_pool.tile([P, CHUNK_GROUPS * K_PASS], BF16, align_bytes=64)
            grouped_words = grouped[:].bitcast(F32)
            for pair in range(CHUNK_GROUPS // 2):
                flipped = work_psum.tile([P, 2, 2, P], F32, tag="work")
                for i in range(2):
                    first = (2 * pair + i) * WORDS_PER_GROUP
                    for u in range(2):
                        nc.tensor.transpose(
                            flipped[:, i, u, :],
                            h_words[:, first + u : first + WORDS_PER_GROUP : 2],
                            identity[:],
                        )
                target = grouped_words[
                    :, 2 * pair * WORDS_PER_GROUP : 2 * (pair + 1) * WORDS_PER_GROUP
                ].rearrange("p (i n u) -> p i n u", i=2, u=2)
                source = flipped[:].rearrange("p i u n -> p i n u")
                if pair % 2 == 0:
                    nc.vector.tensor_copy(out=target, in_=source)
                else:
                    nc.scalar.copy(out=target, in_=source)
            chunk_cols = slice(c * CHUNK_GROUPS * P, (c + 1) * CHUNK_GROUPS * P)
            nc.vector.quantize_mx(
                out=h_codes[:, chunk_cols].bitcast(FP8X4),
                scales=h_planes[:, chunk_cols],
                in_=grouped[:],
            )

        bias = []
        for b in range(BLOCKS):
            bias_b = work_psum.tile([P, F], F32, tag="work")
            nc.tensor.matmul(
                bias_b[:], lhsT=ones[:], rhs=bias_rows[:, b * F : (b + 1) * F],
                start=True, stop=True,
            )
            bias.append(bias_b)
        base_q = keep.tile([P, F], F32)
        gated = keep.tile([P, F], F32)
        nc.vector.tensor_tensor(out=base_q[:], in0=bias[0][:], in1=q_in[:], op=ADD)
        nc.vector.tensor_tensor(out=gated[:], in0=bias[2][:], in1=mu_vw_in[:], op=MULT)
        nc.vector.tensor_tensor(out=base_q[:], in0=base_q[:], in1=gated[:], op=ADD)
        base_mu = keep.tile([P, COMPONENTS, F], F32)
        for x in range(COMPONENTS):
            nc.vector.tensor_tensor(
                out=base_mu[:, x, :], in0=bias[1][:], in1=mu_w_in[:, x, :], op=MULT
            )
            nc.vector.tensor_tensor(
                out=base_mu[:, x, :], in0=base_mu[:, x, :], in1=mu_in[:, x, :], op=ADD
            )

        acc = [acc_psum.tile([P, F], F32, name="acc%d" % b) for b in range(BLOCKS)]

        def mx_pass(g, b, w_words):
            first_row = 4 * (g % PLANES_PER_TILE)
            nc.tensor.matmul_mx(
                out=acc[b][:],
                lhsT=h_codes[:, g * P : (g + 1) * P].bitcast(FP8X4),
                lhsT_scale=h_planes[:, g * P : (g + 1) * P],
                rhs=w_words.bitcast(FP8X4),
                rhs_scale=w_planes[first_row:P, g // PLANES_PER_TILE, b * F : (b + 1) * F],
                start=(g == 0),
                stop=(g == GROUPS - 1),
            )

        for g in range(GROUPS - TAIL_GROUPS):
            w_group = w_pool.tile([P, BLOCKS * F], U32, align_bytes=64)
            if g % 2 == 0:
                nc.sync.dma_start(
                    out=w_group[:].bitcast(I32),
                    in_=W2_words[g].rearrange("p n t -> p (n t)").bitcast(I32),
                )
            else:
                nc.scalar.dma_start(
                    out=w_group[:].bitcast(F32),
                    in_=W2_words[g].rearrange("p n t -> p (n t)").bitcast(F32),
                )
            for b in range(BLOCKS):
                mx_pass(g, b, w_group[:, b * F : (b + 1) * F])

        tail_groups = range(GROUPS - TAIL_GROUPS, GROUPS)
        tail_words = {}
        for b in TAIL_BLOCK_ORDER:
            for g in tail_groups:
                w_part = tail_pool.tile([P, F], U32, align_bytes=64)
                nc.sync.dma_start(
                    out=w_part[:].bitcast(I32),
                    in_=W2_words[g][:, b * F : (b + 1) * F, :]
                    .rearrange("p n t -> p (n t)")
                    .bitcast(I32),
                )
                tail_words[(b, g)] = w_part

        for g in tail_groups:
            mx_pass(g, 1, tail_words[(1, g)][:])
        mu_prod = keep.tile([P, COMPONENTS, F], F32)
        mu_res = keep.tile([P, COMPONENTS, F], F32)
        for x in range(COMPONENTS):
            nc.vector.tensor_tensor(
                out=mu_prod[:, x, :], in0=acc[1][:], in1=mu_w_in[:, x, :], op=MULT
            )
            nc.gpsimd.tensor_tensor(
                out=mu_res[:, x, :], in0=mu_prod[:, x, :], in1=base_mu[:, x, :], op=ADD
            )
            nc.sync.dma_start(out=out_1[:, x, :], in_=mu_res[:, x, :])

        for g in tail_groups:
            mx_pass(g, 2, tail_words[(2, g)][:])
        nc.vector.tensor_tensor(out=gated[:], in0=acc[2][:], in1=mu_vw_in[:], op=MULT)
        nc.vector.tensor_tensor(out=base_q[:], in0=base_q[:], in1=gated[:], op=ADD)

        for g in tail_groups:
            mx_pass(g, 0, tail_words[(0, g)][:])
        q_res = keep.tile([P, F], F32)
        nc.vector.tensor_tensor(out=q_res[:], in0=acc[0][:], in1=base_q[:], op=ADD)
        nc.sync.dma_start(out=out_0.rearrange("n o f -> n (o f)"), in_=q_res[:])
